import numpy as np
import ml_dtypes


def mxq(x, axis, fmt="e4m3"):
    dtype, down = {"e4m3": (ml_dtypes.float8_e4m3fn, 7), "e5m2": (ml_dtypes.float8_e5m2, 14)}[fmt]
    v = np.moveaxis(np.asarray(x, np.float32).astype(ml_dtypes.bfloat16).astype(np.float64), axis, -1)
    blocks = v.reshape(v.shape[:-1] + (-1, 32))
    amax = np.abs(blocks).max(-1, keepdims=True)
    byte = np.maximum(np.where(amax > 0, np.frexp(amax)[1] - 1 + 127, 0) - down, 1)
    scale = np.exp2(byte - 127.0)
    codes = (blocks / scale).astype(np.float32).astype(dtype).astype(np.float64)
    return np.moveaxis((codes * scale).reshape(v.shape), -1, axis)


WIDE = False


def mx_kscale(k):
    if not WIDE:
        return np.ones(k)
    levels = np.array([10, -10, 5, -5, 0])
    if k % 512:
        return np.exp2(np.random.permutation(np.resize(levels, k // 32))).repeat(32)
    a = np.empty((k // 512, 16))
    for p in range(k // 512):
        a[p, :8] = np.random.permutation(np.resize(levels, 8))
        for g in range(8):
            far = levels[np.abs(levels - a[p, g]) >= 10]
            a[p, g + 8] = far[np.random.randint(len(far))]
    return np.exp2(a.ravel()).repeat(32)


BF16 = ml_dtypes.bfloat16


def bf(x):
    return np.asarray(x, np.float32).astype(BF16)


def f64(x):
    return np.asarray(x).astype(np.float64)


T, B, D, U, V, E = 3, 4096, 512, 1024, 16, 8
G = 2 * E


def softmax(v):
    e = np.exp(v - v.max(-1, keepdims=True))
    return e / e.sum(-1, keepdims=True)


def setup_inputs():
    rn = np.random.standard_normal
    s = mx_kscale(U)
    return {
        "task_h": bf(np.abs(rn((T, B, U))) * 0.55 * s),
        "share_h": bf(np.abs(rn((B, U))) * 0.5 * s),
        "ews1": bf(rn((U, V, E)) * 2.0 / np.sqrt(U) / s[:, None, None]),
        "ebs1": bf(rn((V, E)) * 0.5),
        "ew1": bf(rn((T, U, V, E)) * 2.0 / np.sqrt(U) / s[None, :, None, None]),
        "eb1": bf(rn((T, V, E)) * 0.5),
        "gate_pre1": bf(rn((T, B, G))),
        "gb1": bf(rn((T, G)) * 0.5),
    }


def reference(task_h, share_h, ews1, ebs1, ew1, eb1, gate_pre1, gb1):
    es = np.maximum((mxq(f64(share_h), 1, "e4m3") @ mxq(f64(ews1).reshape(U, V * E), 0, "e4m3")).reshape(B, V, E) + f64(ebs1), 0.0)
    et = np.maximum((mxq(f64(task_h), 2, "e4m3") @ mxq(f64(ew1).reshape(T, U, V * E), 1, "e4m3")).reshape(T, B, V, E) + f64(eb1)[:, None], 0.0)
    g = softmax(f64(gate_pre1) + f64(gb1)[:, None])
    comb = np.concatenate([et, np.broadcast_to(es, et.shape)], axis=-1)
    return (comb * g[:, :, None, :]).sum(-1)

@@ -1,0 +1,226 @@
+from contextlib import ExitStack
+
+import concourse.mybir as mybir
+from concourse.masks import make_identity
+
+F32 = mybir.dt.float32
+BF16 = mybir.dt.bfloat16
+U32 = mybir.dt.uint32
+U8 = mybir.dt.uint8
+FP8X4 = mybir.dt.float8_e4m3fn_x4
+ACT = mybir.ActivationFunctionType
+ALU = mybir.AluOpType
+AX = mybir.AxisListType
+
+P = 128
+T, B, U, V, E = 3, 4096, 1024, 16, 8
+G = 2 * E
+C = V * E
+STREAMS = T + 1
+PACK = 4
+K_PASS = P * PACK
+PASSES = U // K_PASS
+ROWS = B // P
+J = 4
+N = J * P
+CHUNKS = ROWS // J
+UNITS = CHUNKS * STREAMS
+WORDS = U // 2
+AHEAD = 5
+
+FLOPS = 2 * STREAMS * B * U * C
+
+
+def tile_plelayer_pb_t_kernel(tc, task_h, share_h, ews1, ebs1, ew1, eb1, gate_pre1, gb1, out):
+    nc = tc.nc
+    stream_rows = [share_h.rearrange("(p j) u -> p (j u)", p=P)]
+    stream_rows += [task_h[t].rearrange("(p j) u -> p (j u)", p=P) for t in range(T)]
+    out_rows = out.rearrange("t (p j) v -> p t (j v)", p=P)
+
+    with ExitStack() as ctx:
+        const = ctx.enter_context(tc.tile_pool(name="const", bufs=1))
+        x_pool = ctx.enter_context(tc.tile_pool(name="x", bufs=AHEAD + 1))
+        mx_pool = ctx.enter_context(tc.tile_pool(name="mx", bufs=3))
+        prod_pool = ctx.enter_context(tc.tile_pool(name="prod", bufs=2 * T))
+        fwd_ps = ctx.enter_context(tc.psum_pool(name="fwd", bufs=4))
+        acc_ps = ctx.enter_context(tc.psum_pool(name="acc", bufs=2))
+        nat_ps = ctx.enter_context(tc.psum_pool(name="nat", bufs=2))
+        ctx.enter_context(tc.manual_schedule())
+
+        x_tiles, grouped_tiles, code_tiles, scale_tiles = {}, {}, {}, {}
+        acc_tiles, relu_tiles, nat_tiles, prod_tiles = {}, {}, {}, {}
+
+        def load(n):
+            chunk, stream = divmod(n, STREAMS)
+            x_tiles[n] = x_pool.tile([P, J * U], BF16, name="x_rows")
+            nc.sync.dma_start(out=x_tiles[n][:], in_=stream_rows[stream][:, chunk * J * U : (chunk + 1) * J * U])
+
+        ident = const.tile([P, P], F32)
+        make_identity(nc, ident[:])
+        bias_rows = const.tile([P, P], BF16)
+        nc.vector.memset(bias_rows[:], 0.0)
+
+        gate_raw = const.tile([P, T * ROWS * G], BF16)
+        nc.sync.dma_start(
+            out=gate_raw[:].rearrange("p (t r) -> p t r", t=T),
+            in_=gate_pre1.rearrange("t (p j) g -> p t (j g)", p=P),
+        )
+        for n in range(AHEAD):
+            load(n)
+        gb_rep = const.tile([P, T * G], BF16)
+        nc.scalar.dma_start(out=gb_rep[:], in_=gb1.rearrange("t g -> (t g)").partition_broadcast(P))
+        nc.scalar.dma_start(out=bias_rows[0:1, :], in_=ebs1.rearrange("v x -> (v x)").unsqueeze(0))
+        nc.scalar.dma_start(out=bias_rows[1:STREAMS, :], in_=eb1.rearrange("t v x -> t (v x)"))
+        w_raw = const.tile([P, STREAMS, PASSES, PACK, C], BF16)
+        nc.scalar.dma_start(
+            out=w_raw[:, 0].rearrange("q g t c -> q g (t c)"),
+            in_=ews1.rearrange("(g q t) v x -> q g (t v x)", g=PASSES, q=P, t=PACK),
+        )
+        nc.scalar.dma_start(
+            out=w_raw[:, 1:STREAMS].rearrange("q s g t c -> q s g (t c)"),
+            in_=ew1.rearrange("s (g q t) v x -> q s g (t v x)", g=PASSES, q=P, t=PACK),
+        )
+
+        gate = const.tile([P, T * ROWS, G], F32)
+        nc.vector.tensor_tensor(
+            out=gate[:].rearrange("p (t j) g -> p t j g", t=T),
+            in0=gate_raw[:].rearrange("p (t j g) -> p t j g", t=T, j=ROWS),
+            in1=gb_rep[:].rearrange("p (t g) -> p t g", t=T).unsqueeze(2).to_broadcast([P, T, ROWS, G]),
+            op=ALU.add,
+        )
+        gate_max = const.tile([P, T * ROWS], F32)
+        nc.vector.tensor_reduce(out=gate_max[:], in_=gate[:], axis=AX.X, op=ALU.max)
+        nc.vector.tensor_tensor(
+            out=gate[:],
+            in0=gate[:],
+            in1=gate_max[:].unsqueeze(2).to_broadcast([P, T * ROWS, G]),
+            op=ALU.subtract,
+        )
+
+        bias_rows_f32 = const.tile([P, P], F32)
+        nc.vector.tensor_copy(out=bias_rows_f32[:], in_=bias_rows[:])
+
+        w_grouped = const.tile([P, STREAMS, PASSES, C, PACK], BF16, align_bytes=64)
+        w_codes = const.tile([P, STREAMS, PASSES, C], U32, align_bytes=64)
+        w_scales = const.tile([P, STREAMS, PASSES, C], U8, align_bytes=64)
+        for s in range(STREAMS):
+            nc.vector.tensor_copy(out=w_grouped[:, s], in_=w_raw[:, s].rearrange("q g t c -> q g c t"))
+        for s in range(STREAMS):
+            nc.vector.quantize_mx(
+                out=w_codes[:, s].rearrange("q g c -> q (g c)").bitcast(FP8X4),
+                scales=w_scales[:, s].rearrange("q g c -> q (g c)"),
+                in_=w_grouped[:, s].rearrange("q g c t -> q (g c t)"),
+            )
+
+        def transpose_in(n):
+            x_words = x_tiles[n][:].bitcast(F32)
+            grouped_tiles[n] = mx_pool.tile([P, PASSES * N * PACK], BF16, name="grouped", align_bytes=64)
+            grouped_words = grouped_tiles[n][:].bitcast(F32).rearrange("q (g c h) -> q g c h", g=PASSES, h=2)
+            for j in range(J):
+                xt = fwd_ps.tile([P, 4, P], F32, name="xt")
+                for g in range(PASSES):
+                    for h in range(2):
+                        first = j * WORDS + g * 2 * P + h
+                        last = j * WORDS + (g + 1) * 2 * P
+                        nc.tensor.transpose(xt[:, 2 * g + h, :], x_words[:, first:last:2], ident[:])
+                nc.scalar.copy(
+                    out=grouped_words[:, :, j * P : (j + 1) * P, :],
+                    in_=xt[:].rearrange("q (g h) r -> q g r h", g=PASSES),
+                )
+
+        def quantise(n):
+            code_tiles[n] = mx_pool.tile([P, PASSES * N], U32, name="codes", align_bytes=64)
+            scale_tiles[n] = mx_pool.tile([P, PASSES * N], U8, name="scales", align_bytes=64)
+            nc.vector.quantize_mx(
+                out=code_tiles[n][:].bitcast(FP8X4), scales=scale_tiles[n][:], in_=grouped_tiles[n][:]
+            )
+
+        def expert_matmul(n):
+            s = n % STREAMS
+            acc_tiles[n] = acc_ps.tile([P, N], F32, name="acc")
+            for g in range(PASSES):
+                nc.tensor.matmul_mx(
+                    out=acc_tiles[n][:],
+                    lhsT=w_codes[:, s, g, :].bitcast(FP8X4),
+                    lhsT_scale=w_scales[:, s, g, :],
+                    rhs=code_tiles[n][:, g * N : (g + 1) * N].bitcast(FP8X4),
+                    rhs_scale=scale_tiles[n][:, g * N : (g + 1) * N],
+                    start=(g == 0),
+                    stop=(g == PASSES - 1),
+                )
+
+        def bias_relu(n):
+            s = n % STREAMS
+            relu_tiles[n] = mx_pool.tile([P, N], F32, name="relu")
+            nc.scalar.activation(
+                out=relu_tiles[n][:], in_=acc_tiles[n][:], func=ACT.Relu, bias=bias_col[:, s : s + 1], scale=1.0
+            )
+
+        def transpose_back(n):
+            nat_tiles[n] = nat_ps.tile([P, J, C], F32, name="nat")
+            for j in range(J):
+                nc.tensor.transpose(nat_tiles[n][:, j, :], relu_tiles[n][:, j * P : (j + 1) * P], ident[:])
+
+        def weigh(n, t, half):
+            chunk = n // STREAMS
+            rows = slice(t * ROWS + chunk * J, t * ROWS + (chunk + 1) * J)
+            nc.vector.tensor_tensor(
+                out=prod_tiles[(chunk, t)][:, :, :, half * E : (half + 1) * E],
+                in0=nat_tiles[n][:].rearrange("p j (v e) -> p j v e", v=V),
+                in1=gate[:, rows, half * E : (half + 1) * E].unsqueeze(2).to_broadcast([P, J, V, E]),
+                op=ALU.mult,
+            )
+
+        def gate_and_sum(n):
+            chunk, s = divmod(n, STREAMS)
+            if s == 0:
+                for t in range(T):
+                    prod_tiles[(chunk, t)] = prod_pool.tile([P, J, V, G], F32, name="prod")
+                    weigh(n, t, 1)
+            else:
+                t = s - 1
+                weigh(n, t, 0)
+                nc.vector.tensor_reduce(
+                    out=out_sb[:, t, chunk * J * V : (chunk + 1) * J * V],
+                    in_=prod_tiles[(chunk, t)][:].rearrange("p j v g -> p (j v) g"),
+                    axis=AX.X,
+                    op=ALU.add,
+                )
+            if s == T:
+                cols = slice(chunk * J * V, (chunk + 1) * J * V)
+                nc.sync.dma_start(out=out_rows[:, :, cols], in_=out_sb[:, :, cols])
+
+        out_sb = const.tile([P, T, ROWS * V], F32)
+
+        transpose_in(0)
+
+        bias_ps = nat_ps.tile([P, J, C], F32, name="nat")
+        nc.tensor.transpose(bias_ps[:, 0, :], bias_rows_f32[:], ident[:])
+        bias_col = const.tile([P, STREAMS], F32)
+        nc.vector.tensor_copy(out=bias_col[:], in_=bias_ps[:, 0, 0:STREAMS])
+
+        nc.scalar.activation(out=gate[:], in_=gate[:], func=ACT.Exp)
+        gate_sum = const.tile([P, T * ROWS], F32)
+        nc.vector.tensor_reduce(out=gate_sum[:], in_=gate[:], axis=AX.X, op=ALU.add)
+        nc.vector.reciprocal(out=gate_sum[:], in_=gate_sum[:])
+        nc.vector.tensor_tensor(
+            out=gate[:],
+            in0=gate[:],
+            in1=gate_sum[:].unsqueeze(2).to_broadcast([P, T * ROWS, G]),
+            op=ALU.mult,
+        )
+
+        for step in range(1, UNITS + 3):
+            if step + AHEAD - 1 < UNITS:
+                load(step + AHEAD - 1)
+            if step - 1 < UNITS:
+                quantise(step - 1)
+            if 0 <= step - 2 < UNITS:
+                expert_matmul(step - 2)
+                bias_relu(step - 2)
+            if step < UNITS:
+                transpose_in(step)
+            if 0 <= step - 2 < UNITS:
+                transpose_back(step - 2)
+            if 0 <= step - 3:
+                gate_and_sum(step - 3)

@@ -41,7 +41,7 @@ def tile_plelayer_pb_t_kernel(tc, task_h, share_h, ews1, ebs1, ew1, eb1, gate_pr
         const = ctx.enter_context(tc.tile_pool(name="const", bufs=1))
         x_pool = ctx.enter_context(tc.tile_pool(name="x", bufs=AHEAD + 1))
         mx_pool = ctx.enter_context(tc.tile_pool(name="mx", bufs=3))
-        prod_pool = ctx.enter_context(tc.tile_pool(name="prod", bufs=2 * T))
+        prod_pool = ctx.enter_context(tc.tile_pool(name="prod", bufs=2))
         fwd_ps = ctx.enter_context(tc.psum_pool(name="fwd", bufs=4))
         acc_ps = ctx.enter_context(tc.psum_pool(name="acc", bufs=2))
         nat_ps = ctx.enter_context(tc.psum_pool(name="nat", bufs=2))
@@ -50,67 +50,40 @@ def tile_plelayer_pb_t_kernel(tc, task_h, share_h, ews1, ebs1, ew1, eb1, gate_pr
         x_tiles, grouped_tiles, code_tiles, scale_tiles = {}, {}, {}, {}
         acc_tiles, relu_tiles, nat_tiles, prod_tiles = {}, {}, {}, {}
 
-        def load(n):
+        def load(n, pieces=1):
             chunk, stream = divmod(n, STREAMS)
             x_tiles[n] = x_pool.tile([P, J * U], BF16, name="x_rows")
-            nc.sync.dma_start(out=x_tiles[n][:], in_=stream_rows[stream][:, chunk * J * U : (chunk + 1) * J * U])
+            width = J * U // pieces
+            for i in range(pieces):
+                first = chunk * J * U + i * width
+                nc.sync.dma_start(
+                    out=x_tiles[n][:, i * width : (i + 1) * width], in_=stream_rows[stream][:, first : first + width]
+                )
 
+        warm = const.tile([P, 1], F32)
+        nc.gpsimd.memset(warm[:], 0.0)
+        nc.scalar.activation(out=warm[:], in_=warm[:], func=ACT.Exp)
         ident = const.tile([P, P], F32)
         make_identity(nc, ident[:])
+        load(0, pieces=2)
+        gate_raw = const.tile([P, T, ROWS * G], BF16)
         bias_rows = const.tile([P, P], BF16)
         nc.vector.memset(bias_rows[:], 0.0)
-
-        gate_raw = const.tile([P, T * ROWS * G], BF16)
-        nc.sync.dma_start(
-            out=gate_raw[:].rearrange("p (t r) -> p t r", t=T),
-            in_=gate_pre1.rearrange("t (p j) g -> p t (j g)", p=P),
-        )
-        for n in range(AHEAD):
-            load(n)
-        gb_rep = const.tile([P, T * G], BF16)
-        nc.scalar.dma_start(out=gb_rep[:], in_=gb1.rearrange("t g -> (t g)").partition_broadcast(P))
+        gate_bias_row = const.tile([P, T * G], BF16)
+        nc.vector.memset(gate_bias_row[:], 0.0)
+        nc.scalar.dma_start(out=gate_bias_row[0:1, :], in_=gb1.rearrange("t g -> (t g)").unsqueeze(0))
         nc.scalar.dma_start(out=bias_rows[0:1, :], in_=ebs1.rearrange("v x -> (v x)").unsqueeze(0))
         nc.scalar.dma_start(out=bias_rows[1:STREAMS, :], in_=eb1.rearrange("t v x -> t (v x)"))
         w_raw = const.tile([P, STREAMS, PASSES, PACK, C], BF16)
-        nc.scalar.dma_start(
-            out=w_raw[:, 0].rearrange("q g t c -> q g (t c)"),
-            in_=ews1.rearrange("(g q t) v x -> q g (t v x)", g=PASSES, q=P, t=PACK),
-        )
-        nc.scalar.dma_start(
-            out=w_raw[:, 1:STREAMS].rearrange("q s g t c -> q s g (t c)"),
-            in_=ew1.rearrange("s (g q t) v x -> q s g (t v x)", g=PASSES, q=P, t=PACK),
-        )
-
-        gate = const.tile([P, T * ROWS, G], F32)
-        nc.vector.tensor_tensor(
-            out=gate[:].rearrange("p (t j) g -> p t j g", t=T),
-            in0=gate_raw[:].rearrange("p (t j g) -> p t j g", t=T, j=ROWS),
-            in1=gb_rep[:].rearrange("p (t g) -> p t g", t=T).unsqueeze(2).to_broadcast([P, T, ROWS, G]),
-            op=ALU.add,
-        )
-        gate_max = const.tile([P, T * ROWS], F32)
-        nc.vector.tensor_reduce(out=gate_max[:], in_=gate[:], axis=AX.X, op=ALU.max)
-        nc.vector.tensor_tensor(
-            out=gate[:],
-            in0=gate[:],
-            in1=gate_max[:].unsqueeze(2).to_broadcast([P, T * ROWS, G]),
-            op=ALU.subtract,
-        )
-
-        bias_rows_f32 = const.tile([P, P], F32)
-        nc.vector.tensor_copy(out=bias_rows_f32[:], in_=bias_rows[:])
-
-        w_grouped = const.tile([P, STREAMS, PASSES, C, PACK], BF16, align_bytes=64)
-        w_codes = const.tile([P, STREAMS, PASSES, C], U32, align_bytes=64)
-        w_scales = const.tile([P, STREAMS, PASSES, C], U8, align_bytes=64)
         for s in range(STREAMS):
-            nc.vector.tensor_copy(out=w_grouped[:, s], in_=w_raw[:, s].rearrange("q g t c -> q g c t"))
-        for s in range(STREAMS):
-            nc.vector.quantize_mx(
-                out=w_codes[:, s].rearrange("q g c -> q (g c)").bitcast(FP8X4),
-                scales=w_scales[:, s].rearrange("q g c -> q (g c)"),
-                in_=w_grouped[:, s].rearrange("q g c t -> q (g c t)"),
+            w_hbm = ews1 if s == 0 else ew1[s - 1]
+            nc.sync.dma_start(
+                out=w_raw[:, s].rearrange("q g t c -> q g (t c)"),
+                in_=w_hbm.rearrange("(g q t) v x -> q g (t v x)", g=PASSES, q=P, t=PACK),
             )
+            if s == 0:
+                nc.sync.dma_start(out=gate_raw[:], in_=gate_pre1.rearrange("t (p j) g -> p t (j g)", p=P))
+            load(s + 1)
 
         def transpose_in(n):
             x_words = x_tiles[n][:].bitcast(F32)
@@ -161,66 +134,158 @@ def tile_plelayer_pb_t_kernel(tc, task_h, share_h, ews1, ebs1, ew1, eb1, gate_pr
             for j in range(J):
                 nc.tensor.transpose(nat_tiles[n][:, j, :], relu_tiles[n][:, j * P : (j + 1) * P], ident[:])
 
-        def weigh(n, t, half):
-            chunk = n // STREAMS
-            rows = slice(t * ROWS + chunk * J, t * ROWS + (chunk + 1) * J)
-            nc.vector.tensor_tensor(
-                out=prod_tiles[(chunk, t)][:, :, :, half * E : (half + 1) * E],
-                in0=nat_tiles[n][:].rearrange("p j (v e) -> p j v e", v=V),
-                in1=gate[:, rows, half * E : (half + 1) * E].unsqueeze(2).to_broadcast([P, J, V, E]),
-                op=ALU.mult,
-            )
+        def weigh(n):
+            chunk, s = divmod(n, STREAMS)
+            values = nat_tiles[n][:].rearrange("p j (v e) -> p j v e", v=V)
+            if s == 0:
+                prod_tiles[chunk] = prod_pool.tile([P, T, J, V, G], F32, name="prod")
+                nc.vector.tensor_tensor(
+                    out=prod_tiles[chunk][:, :, :, :, E:G],
+                    in0=values.unsqueeze(1).to_broadcast([P, T, J, V, E]),
+                    in1=gate[:, chunk, 1].unsqueeze(3).to_broadcast([P, T, J, V, E]),
+                    op=ALU.mult,
+                )
+            else:
+                nc.vector.tensor_tensor(
+                    out=prod_tiles[chunk][:, s - 1, :, :, 0:E],
+                    in0=values,
+                    in1=gate[:, chunk, 0, s - 1].unsqueeze(2).to_broadcast([P, J, V, E]),
+                    op=ALU.mult,
+                )
 
-        def gate_and_sum(n):
+        def sum_experts(n):
             chunk, s = divmod(n, STREAMS)
             if s == 0:
-                for t in range(T):
-                    prod_tiles[(chunk, t)] = prod_pool.tile([P, J, V, G], F32, name="prod")
-                    weigh(n, t, 1)
-            else:
-                t = s - 1
-                weigh(n, t, 0)
-                nc.vector.tensor_reduce(
-                    out=out_sb[:, t, chunk * J * V : (chunk + 1) * J * V],
-                    in_=prod_tiles[(chunk, t)][:].rearrange("p j v g -> p (j v) g"),
-                    axis=AX.X,
-                    op=ALU.add,
-                )
+                return
+            cols = slice(chunk * J * V, (chunk + 1) * J * V)
+            nc.vector.tensor_reduce(
+                out=out_sb[:, s - 1, cols],
+                in_=prod_tiles[chunk][:, s - 1].rearrange("p j v g -> p (j v) g"),
+                axis=AX.X,
+                op=ALU.add,
+            )
             if s == T:
-                cols = slice(chunk * J * V, (chunk + 1) * J * V)
                 nc.sync.dma_start(out=out_rows[:, :, cols], in_=out_sb[:, :, cols])
 
         out_sb = const.tile([P, T, ROWS * V], F32)
 
         transpose_in(0)
 
+        ones = const.tile([P, P], BF16)
+        nc.vector.memset(ones[:], 1.0)
+        gb_ps = acc_ps.tile([P, N], F32, name="acc")
+        nc.tensor.matmul(gb_ps[:, 0 : T * G], lhsT=ones[:], rhs=gate_bias_row[:], start=True, stop=True)
+        gate_bias = const.tile([P, T, G], F32)
+        nc.vector.tensor_copy(out=gate_bias[:].rearrange("p t g -> p (t g)"), in_=gb_ps[:, 0 : T * G])
+        bias_rows_f32 = const.tile([P, P], F32)
+        nc.vector.tensor_copy(out=bias_rows_f32[:], in_=bias_rows[:])
         bias_ps = nat_ps.tile([P, J, C], F32, name="nat")
         nc.tensor.transpose(bias_ps[:, 0, :], bias_rows_f32[:], ident[:])
         bias_col = const.tile([P, STREAMS], F32)
         nc.vector.tensor_copy(out=bias_col[:], in_=bias_ps[:, 0, 0:STREAMS])
 
-        nc.scalar.activation(out=gate[:], in_=gate[:], func=ACT.Exp)
-        gate_sum = const.tile([P, T * ROWS], F32)
-        nc.vector.tensor_reduce(out=gate_sum[:], in_=gate[:], axis=AX.X, op=ALU.add)
-        nc.vector.reciprocal(out=gate_sum[:], in_=gate_sum[:])
-        nc.vector.tensor_tensor(
-            out=gate[:],
-            in0=gate[:],
-            in1=gate_sum[:].unsqueeze(2).to_broadcast([P, T * ROWS, G]),
-            op=ALU.mult,
-        )
+        logits = const.tile([P, CHUNKS, T, J, G], F32)
+        gate = const.tile([P, CHUNKS, 2, T, J, E], F32)
+        gate_max = const.tile([P, CHUNKS * T * J], F32)
+        gate_sum = const.tile([P, CHUNKS * T * J], F32)
 
-        for step in range(1, UNITS + 3):
+        def gate_rows(tile, first, last):
+            return tile[:, first * T * J : last * T * J].unsqueeze(2).to_broadcast([P, (last - first) * T * J, G])
+
+        def gate_logits(eng, first, last):
+            for t in range(T):
+                eng.tensor_tensor(
+                    out=logits[:, first:last, t],
+                    in0=gate_raw[:, t, first * J * G : last * J * G].rearrange("p (c j g) -> p c j g", j=J, g=G),
+                    in1=gate_bias[:, t, :].unsqueeze(1).unsqueeze(1).to_broadcast([P, last - first, J, G]),
+                    op=ALU.add,
+                )
+
+        def flat_logits(first, last):
+            return logits[:, first:last].rearrange("p c t j g -> p (c t j) g")
+
+        def gate_maximum(first, last):
+            nc.vector.tensor_reduce(
+                out=gate_max[:, first * T * J : last * T * J], in_=flat_logits(first, last), axis=AX.X, op=ALU.max
+            )
+
+        def gate_shift(eng, first, last):
+            eng.tensor_tensor(
+                out=flat_logits(first, last),
+                in0=flat_logits(first, last),
+                in1=gate_rows(gate_max, first, last),
+                op=ALU.subtract,
+            )
+
+        def gate_exp(first, last):
+            nc.scalar.activation(out=flat_logits(first, last), in_=flat_logits(first, last), func=ACT.Exp)
+
+        def gate_total(first, last):
+            rows = slice(first * T * J, last * T * J)
+            nc.vector.tensor_reduce(out=gate_sum[:, rows], in_=flat_logits(first, last), axis=AX.X, op=ALU.add)
+            nc.vector.reciprocal(out=gate_sum[:, rows], in_=gate_sum[:, rows])
+
+        def gate_divide(eng, first, last):
+            for half in range(2):
+                eng.tensor_tensor(
+                    out=gate[:, first:last, half].rearrange("p c t j e -> p c (t j) e"),
+                    in0=logits[:, first:last, :, :, half * E : (half + 1) * E].rearrange("p c t j e -> p c (t j) e"),
+                    in1=gate_sum[:, first * T * J : last * T * J]
+                    .rearrange("p (c r) -> p c r", r=T * J)
+                    .unsqueeze(3)
+                    .to_broadcast([P, last - first, T * J, E]),
+                    op=ALU.mult,
+                )
+
+        w_grouped = const.tile([P, STREAMS, PASSES, C, PACK], BF16, align_bytes=64)
+        w_codes = const.tile([P, STREAMS, PASSES, C], U32, align_bytes=64)
+        w_scales = const.tile([P, STREAMS, PASSES, C], U8, align_bytes=64)
+
+        def group_weights(s, copy=nc.scalar.copy):
+            copy(out=w_grouped[:, s], in_=w_raw[:, s].rearrange("q g t c -> q g c t"))
+
+        def quantise_weights(s):
+            nc.vector.quantize_mx(
+                out=w_codes[:, s].rearrange("q g c -> q (g c)").bitcast(FP8X4),
+                scales=w_scales[:, s].rearrange("q g c -> q (g c)"),
+                in_=w_grouped[:, s].rearrange("q g c t -> q (g c t)"),
+            )
+
+        group_weights(0, nc.vector.tensor_copy)
+        gate_logits(nc.vector, 0, 1)
+        quantise_weights(0)
+        gate_maximum(0, 1)
+        gate_logits(nc.gpsimd, 1, CHUNKS)
+        gate_shift(nc.vector, 0, 1)
+        gate_exp(0, 1)
+
+        for step in range(1, UNITS + 4):
             if step + AHEAD - 1 < UNITS:
                 load(step + AHEAD - 1)
-            if step - 1 < UNITS:
-                quantise(step - 1)
             if 0 <= step - 2 < UNITS:
-                expert_matmul(step - 2)
                 bias_relu(step - 2)
+            if step < STREAMS:
+                group_weights(step)
             if step < UNITS:
                 transpose_in(step)
             if 0 <= step - 2 < UNITS:
                 transpose_back(step - 2)
-            if 0 <= step - 3:
-                gate_and_sum(step - 3)
+            if step - 1 < UNITS:
+                quantise(step - 1)
+                expert_matmul(step - 1)
+            if step == 1:
+                gate_total(0, 1)
+                gate_divide(nc.vector, 0, 1)
+                gate_maximum(1, CHUNKS)
+                gate_shift(nc.gpsimd, 1, CHUNKS)
+            if step < STREAMS:
+                quantise_weights(step)
+            if step == 3:
+                gate_exp(1, CHUNKS)
+            if step == 4:
+                gate_total(1, CHUNKS)
+                gate_divide(nc.gpsimd, 1, CHUNKS)
+            if 0 <= step - 4:
+                sum_experts(step - 4)
+            if 0 <= step - 3 < UNITS:
+                weigh(step - 3)

@@ -60,30 +60,38 @@ def tile_plelayer_pb_t_kernel(tc, task_h, share_h, ews1, ebs1, ew1, eb1, gate_pr
                     out=x_tiles[n][:, i * width : (i + 1) * width], in_=stream_rows[stream][:, first : first + width]
                 )
 
+        bias_rows = const.tile([P, P], BF16)
+        nc.vector.memset(bias_rows[:], 0.0)
+        gate_bias_row = const.tile([P, T * G], BF16)
+        nc.vector.memset(gate_bias_row[:], 0.0)
+        nc.scalar.dma_start(out=bias_rows[0:1, :], in_=ebs1.rearrange("v x -> (v x)").unsqueeze(0))
+        nc.scalar.dma_start(out=bias_rows[1:STREAMS, :], in_=eb1.rearrange("t v x -> t (v x)"))
+        nc.scalar.dma_start(out=gate_bias_row[0:1, :], in_=gb1.rearrange("t g -> (t g)").unsqueeze(0))
         warm = const.tile([P, 1], F32)
         nc.gpsimd.memset(warm[:], 0.0)
         nc.scalar.activation(out=warm[:], in_=warm[:], func=ACT.Exp)
         ident = const.tile([P, P], F32)
         make_identity(nc, ident[:])
-        load(0, pieces=2)
-        gate_raw = const.tile([P, T, ROWS * G], BF16)
-        bias_rows = const.tile([P, P], BF16)
-        nc.vector.memset(bias_rows[:], 0.0)
-        gate_bias_row = const.tile([P, T * G], BF16)
-        nc.vector.memset(gate_bias_row[:], 0.0)
-        nc.scalar.dma_start(out=gate_bias_row[0:1, :], in_=gb1.rearrange("t g -> (t g)").unsqueeze(0))
-        nc.scalar.dma_start(out=bias_rows[0:1, :], in_=ebs1.rearrange("v x -> (v x)").unsqueeze(0))
-        nc.scalar.dma_start(out=bias_rows[1:STREAMS, :], in_=eb1.rearrange("t v x -> t (v x)"))
         w_raw = const.tile([P, STREAMS, PASSES, PACK, C], BF16)
-        for s in range(STREAMS):
+
+        def load_weights(s):
             w_hbm = ews1 if s == 0 else ew1[s - 1]
             nc.sync.dma_start(
                 out=w_raw[:, s].rearrange("q g t c -> q g (t c)"),
                 in_=w_hbm.rearrange("(g q t) v x -> q g (t v x)", g=PASSES, q=P, t=PACK),
             )
-            if s == 0:
-                nc.sync.dma_start(out=gate_raw[:], in_=gate_pre1.rearrange("t (p j) g -> p t (j g)", p=P))
-            load(s + 1)
+
+        load(0, pieces=J)
+        load(1)
+        load_weights(0)
+        load_weights(1)
+        load(2)
+        gate_raw = const.tile([P, T, ROWS * G], BF16)
+        nc.sync.dma_start(out=gate_raw[:], in_=gate_pre1.rearrange("t (p j) g -> p t (j g)", p=P))
+        load_weights(2)
+        load(3)
+        load_weights(3)
+        load(4)
 
         def transpose_in(n):
             x_words = x_tiles[n][:].bitcast(F32)
@@ -164,25 +172,27 @@ def tile_plelayer_pb_t_kernel(tc, task_h, share_h, ews1, ebs1, ew1, eb1, gate_pr
                 axis=AX.X,
                 op=ALU.add,
             )
-            if s == T:
+            if chunk == CHUNKS - 1:
+                nc.sync.dma_start(out=out_rows[:, s - 1, cols], in_=out_sb[:, s - 1, cols])
+            elif s == T:
                 nc.sync.dma_start(out=out_rows[:, :, cols], in_=out_sb[:, :, cols])
 
         out_sb = const.tile([P, T, ROWS * V], F32)
 
-        transpose_in(0)
-
+        gate_bias = const.tile([P, T, G], F32)
+        bias_col = const.tile([P, STREAMS], F32)
         ones = const.tile([P, P], BF16)
         nc.vector.memset(ones[:], 1.0)
-        gb_ps = acc_ps.tile([P, N], F32, name="acc")
-        nc.tensor.matmul(gb_ps[:, 0 : T * G], lhsT=ones[:], rhs=gate_bias_row[:], start=True, stop=True)
-        gate_bias = const.tile([P, T, G], F32)
-        nc.vector.tensor_copy(out=gate_bias[:].rearrange("p t g -> p (t g)"), in_=gb_ps[:, 0 : T * G])
         bias_rows_f32 = const.tile([P, P], F32)
-        nc.vector.tensor_copy(out=bias_rows_f32[:], in_=bias_rows[:])
-        bias_ps = nat_ps.tile([P, J, C], F32, name="nat")
-        nc.tensor.transpose(bias_ps[:, 0, :], bias_rows_f32[:], ident[:])
-        bias_col = const.tile([P, STREAMS], F32)
-        nc.vector.tensor_copy(out=bias_col[:], in_=bias_ps[:, 0, 0:STREAMS])
+
+        def spread_biases():
+            nc.vector.tensor_copy(out=bias_rows_f32[:], in_=bias_rows[:])
+            gb_ps = acc_ps.tile([P, N], F32, name="acc")
+            nc.tensor.matmul(gb_ps[:, 0 : T * G], lhsT=ones[:], rhs=gate_bias_row[:], start=True, stop=True)
+            bias_ps = nat_ps.tile([P, J, C], F32, name="nat")
+            nc.tensor.transpose(bias_ps[:, 0, :], bias_rows_f32[:], ident[:])
+            nc.vector.tensor_copy(out=bias_col[:], in_=bias_ps[:, 0, 0:STREAMS])
+            nc.vector.tensor_copy(out=gate_bias[:].rearrange("p t g -> p (t g)"), in_=gb_ps[:, 0 : T * G])
 
         logits = const.tile([P, CHUNKS, T, J, G], F32)
         gate = const.tile([P, CHUNKS, 2, T, J, E], F32)
@@ -251,41 +261,51 @@ def tile_plelayer_pb_t_kernel(tc, task_h, share_h, ews1, ebs1, ew1, eb1, gate_pr
                 in_=w_grouped[:, s].rearrange("q g c t -> q (g c t)"),
             )
 
-        group_weights(0, nc.vector.tensor_copy)
-        gate_logits(nc.vector, 0, 1)
-        quantise_weights(0)
-        gate_maximum(0, 1)
-        gate_logits(nc.gpsimd, 1, CHUNKS)
-        gate_shift(nc.vector, 0, 1)
-        gate_exp(0, 1)
-
-        for step in range(1, UNITS + 4):
-            if step + AHEAD - 1 < UNITS:
+        for step in range(UNITS + 2):
+            if step > 0 and step + AHEAD - 1 < UNITS:
                 load(step + AHEAD - 1)
-            if 0 <= step - 2 < UNITS:
+            if 0 <= step - 2:
                 bias_relu(step - 2)
-            if step < STREAMS:
-                group_weights(step)
             if step < UNITS:
                 transpose_in(step)
-            if 0 <= step - 2 < UNITS:
+            if 0 <= step - 2:
                 transpose_back(step - 2)
-            if step - 1 < UNITS:
+            if 0 <= step - 1 < UNITS:
                 quantise(step - 1)
-                expert_matmul(step - 1)
             if step == 1:
+                group_weights(0, nc.vector.tensor_copy)
+                spread_biases()
+            if 1 <= step <= STREAMS:
+                quantise_weights(step - 1)
+            if 0 <= step - 1 < UNITS:
+                expert_matmul(step - 1)
+            if step == 2:
+                gate_logits(nc.vector, 0, 1)
+                gate_logits(nc.gpsimd, 1, CHUNKS)
+                gate_maximum(0, 1)
+                gate_shift(nc.vector, 0, 1)
+                gate_exp(0, 1)
+            if 1 <= step < STREAMS:
+                group_weights(step)
+            if step == 3:
                 gate_total(0, 1)
                 gate_divide(nc.vector, 0, 1)
                 gate_maximum(1, CHUNKS)
                 gate_shift(nc.gpsimd, 1, CHUNKS)
-            if step < STREAMS:
-                quantise_weights(step)
-            if step == 3:
+            if step == 5:
                 gate_exp(1, CHUNKS)
-            if step == 4:
+            if step == 6:
                 gate_total(1, CHUNKS)
                 gate_divide(nc.gpsimd, 1, CHUNKS)
-            if 0 <= step - 4:
+            closer = step > UNITS - STREAMS
+            if closer and step == UNITS - STREAMS + 1:
                 sum_experts(step - 4)
-            if 0 <= step - 3 < UNITS:
-                weigh(step - 3)
+            sum_unit, weigh_unit = (step - 3, step - 2) if closer else (step - 4, step - 3)
+            if step == UNITS - STREAMS:
+                weigh(weigh_unit)
+                weigh_unit += 1
+            if 0 <= sum_unit:
+                sum_experts(sum_unit)
+            if 0 <= weigh_unit:
+                weigh(weigh_unit)
+        sum_experts(UNITS - 1)

@@ -22,9 +22,10 @@ K_PASS = P * PACK
 PASSES = U // K_PASS
 ROWS = B // P
 J = 4
-N = J * P
 CHUNKS = ROWS // J
-UNITS = CHUNKS * STREAMS
+WHOLE_UNITS = [(c, s, 0, J) for c in range(CHUNKS) for s in range(STREAMS)][:-1]
+UNIT_LIST = WHOLE_UNITS + [(CHUNKS - 1, T, 0, J // 2), (CHUNKS - 1, T, J // 2, J)]
+UNITS = len(UNIT_LIST)
 WORDS = U // 2
 AHEAD = 5
 
@@ -40,7 +41,7 @@ def tile_plelayer_pb_t_kernel(tc, task_h, share_h, ews1, ebs1, ew1, eb1, gate_pr
     with ExitStack() as ctx:
         const = ctx.enter_context(tc.tile_pool(name="const", bufs=1))
         x_pool = ctx.enter_context(tc.tile_pool(name="x", bufs=AHEAD + 1))
-        mx_pool = ctx.enter_context(tc.tile_pool(name="mx", bufs=3))
+        mx_pool = ctx.enter_context(tc.tile_pool(name="mx", bufs=4))
         prod_pool = ctx.enter_context(tc.tile_pool(name="prod", bufs=2))
         fwd_ps = ctx.enter_context(tc.psum_pool(name="fwd", bufs=4))
         acc_ps = ctx.enter_context(tc.psum_pool(name="acc", bufs=2))
@@ -48,14 +49,14 @@ def tile_plelayer_pb_t_kernel(tc, task_h, share_h, ews1, ebs1, ew1, eb1, gate_pr
         ctx.enter_context(tc.manual_schedule())
 
         x_tiles, grouped_tiles, code_tiles, scale_tiles = {}, {}, {}, {}
-        acc_tiles, relu_tiles, nat_tiles, prod_tiles = {}, {}, {}, {}
+        acc_tiles, relu_tiles, nat_tiles, own_tiles, shared_tiles = {}, {}, {}, {}, {}
 
         def load(n, pieces=1):
-            chunk, stream = divmod(n, STREAMS)
+            chunk, stream, row, end = UNIT_LIST[n]
             x_tiles[n] = x_pool.tile([P, J * U], BF16, name="x_rows")
-            width = J * U // pieces
+            width = (end - row) * U // pieces
             for i in range(pieces):
-                first = chunk * J * U + i * width
+                first = (chunk * J + row) * U + i * width
                 nc.sync.dma_start(
                     out=x_tiles[n][:, i * width : (i + 1) * width], in_=stream_rows[stream][:, first : first + width]
                 )
@@ -93,11 +94,16 @@ def tile_plelayer_pb_t_kernel(tc, task_h, share_h, ews1, ebs1, ew1, eb1, gate_pr
         load_weights(3)
         load(4)
 
+        def rows_of(n):
+            return UNIT_LIST[n][3] - UNIT_LIST[n][2]
+
         def transpose_in(n):
             x_words = x_tiles[n][:].bitcast(F32)
-            grouped_tiles[n] = mx_pool.tile([P, PASSES * N * PACK], BF16, name="grouped", align_bytes=64)
-            grouped_words = grouped_tiles[n][:].bitcast(F32).rearrange("q (g c h) -> q g c h", g=PASSES, h=2)
-            for j in range(J):
+            grouped_tiles[n] = mx_pool.tile([P, PASSES * J * P * PACK], BF16, name="grouped", align_bytes=64)
+            cols = rows_of(n) * P
+            grouped_words = grouped_tiles[n][:, 0 : PASSES * cols * PACK].bitcast(F32)
+            grouped_words = grouped_words.rearrange("q (g c h) -> q g c h", g=PASSES, h=2)
+            for j in range(rows_of(n)):
                 xt = fwd_ps.tile([P, 4, P], F32, name="xt")
                 for g in range(PASSES):
                     for h in range(2):
@@ -110,65 +116,79 @@ def tile_plelayer_pb_t_kernel(tc, task_h, share_h, ews1, ebs1, ew1, eb1, gate_pr
                 )
 
         def quantise(n):
-            code_tiles[n] = mx_pool.tile([P, PASSES * N], U32, name="codes", align_bytes=64)
-            scale_tiles[n] = mx_pool.tile([P, PASSES * N], U8, name="scales", align_bytes=64)
+            code_tiles[n] = mx_pool.tile([P, PASSES * J * P], U32, name="codes", align_bytes=64)
+            scale_tiles[n] = mx_pool.tile([P, PASSES * J * P], U8, name="scales", align_bytes=64)
+            cols = PASSES * rows_of(n) * P
             nc.vector.quantize_mx(
-                out=code_tiles[n][:].bitcast(FP8X4), scales=scale_tiles[n][:], in_=grouped_tiles[n][:]
+                out=code_tiles[n][:, 0:cols].bitcast(FP8X4),
+                scales=scale_tiles[n][:, 0:cols],
+                in_=grouped_tiles[n][:, 0 : cols * PACK],
             )
 
         def expert_matmul(n):
-            s = n % STREAMS
-            acc_tiles[n] = acc_ps.tile([P, N], F32, name="acc")
+            s = UNIT_LIST[n][1]
+            cols = rows_of(n) * P
+            acc_tiles[n] = acc_ps.tile([P, J * P], F32, name="acc")
             for g in range(PASSES):
                 nc.tensor.matmul_mx(
-                    out=acc_tiles[n][:],
+                    out=acc_tiles[n][:, 0:cols],
                     lhsT=w_codes[:, s, g, :].bitcast(FP8X4),
                     lhsT_scale=w_scales[:, s, g, :],
-                    rhs=code_tiles[n][:, g * N : (g + 1) * N].bitcast(FP8X4),
-                    rhs_scale=scale_tiles[n][:, g * N : (g + 1) * N],
+                    rhs=code_tiles[n][:, g * cols : (g + 1) * cols].bitcast(FP8X4),
+                    rhs_scale=scale_tiles[n][:, g * cols : (g + 1) * cols],
                     start=(g == 0),
                     stop=(g == PASSES - 1),
                 )
 
         def bias_relu(n):
-            s = n % STREAMS
-            relu_tiles[n] = mx_pool.tile([P, N], F32, name="relu")
+            s = UNIT_LIST[n][1]
+            cols = rows_of(n) * P
+            relu_tiles[n] = mx_pool.tile([P, J * P], F32, name="relu")
             nc.scalar.activation(
-                out=relu_tiles[n][:], in_=acc_tiles[n][:], func=ACT.Relu, bias=bias_col[:, s : s + 1], scale=1.0
+                out=relu_tiles[n][:, 0:cols],
+                in_=acc_tiles[n][:, 0:cols],
+                func=ACT.Relu,
+                bias=bias_col[:, s : s + 1],
+                scale=1.0,
             )
 
         def transpose_back(n):
             nat_tiles[n] = nat_ps.tile([P, J, C], F32, name="nat")
-            for j in range(J):
+            for j in range(rows_of(n)):
                 nc.tensor.transpose(nat_tiles[n][:, j, :], relu_tiles[n][:, j * P : (j + 1) * P], ident[:])
 
         def weigh(n):
-            chunk, s = divmod(n, STREAMS)
-            values = nat_tiles[n][:].rearrange("p j (v e) -> p j v e", v=V)
+            chunk, s, row, end = UNIT_LIST[n]
+            values = nat_tiles[n][:, 0 : end - row].rearrange("p j (v e) -> p j v e", v=V)
             if s == 0:
-                prod_tiles[chunk] = prod_pool.tile([P, T, J, V, G], F32, name="prod")
+                own_tiles[chunk] = prod_pool.tile([P, T, J, V, E], F32, name="own")
+                shared_tiles[chunk] = prod_pool.tile([P, T, J, V, E], F32, name="shared")
                 nc.vector.tensor_tensor(
-                    out=prod_tiles[chunk][:, :, :, :, E:G],
+                    out=shared_tiles[chunk][:],
                     in0=values.unsqueeze(1).to_broadcast([P, T, J, V, E]),
                     in1=gate[:, chunk, 1].unsqueeze(3).to_broadcast([P, T, J, V, E]),
                     op=ALU.mult,
                 )
             else:
+                own = own_tiles[chunk][:, s - 1, row:end]
                 nc.vector.tensor_tensor(
-                    out=prod_tiles[chunk][:, s - 1, :, :, 0:E],
+                    out=own,
                     in0=values,
-                    in1=gate[:, chunk, 0, s - 1].unsqueeze(2).to_broadcast([P, J, V, E]),
+                    in1=gate[:, chunk, 0, s - 1, row:end].unsqueeze(2).to_broadcast([P, end - row, V, E]),
                     op=ALU.mult,
                 )
+                own = own.rearrange("p j v e -> p (j v e)")
+                shared = shared_tiles[chunk][:, s - 1, row:end].rearrange("p j v e -> p (j v e)")
+                nc.gpsimd.tensor_tensor(out=own, in0=own, in1=shared, op=ALU.add)
 
         def sum_experts(n):
-            chunk, s = divmod(n, STREAMS)
+            chunk, s, row, end = UNIT_LIST[n]
             if s == 0:
                 return
-            cols = slice(chunk * J * V, (chunk + 1) * J * V)
+            cols = slice((chunk * J + row) * V, (chunk * J + end) * V)
             nc.vector.tensor_reduce(
                 out=out_sb[:, s - 1, cols],
-                in_=prod_tiles[chunk][:, s - 1].rearrange("p j v g -> p (j v) g"),
+                in_=own_tiles[chunk][:, s - 1, row:end].rearrange("p j v e -> p (j v) e"),
                 axis=AX.X,
                 op=ALU.add,
             )
@@ -187,7 +207,7 @@ def tile_plelayer_pb_t_kernel(tc, task_h, share_h, ews1, ebs1, ew1, eb1, gate_pr
 
         def spread_biases():
             nc.vector.tensor_copy(out=bias_rows_f32[:], in_=bias_rows[:])
-            gb_ps = acc_ps.tile([P, N], F32, name="acc")
+            gb_ps = acc_ps.tile([P, J * P], F32, name="acc")
             nc.tensor.matmul(gb_ps[:, 0 : T * G], lhsT=ones[:], rhs=gate_bias_row[:], start=True, stop=True)
             bias_ps = nat_ps.tile([P, J, C], F32, name="nat")
             nc.tensor.transpose(bias_ps[:, 0, :], bias_rows_f32[:], ident[:])
@@ -261,24 +281,46 @@ def tile_plelayer_pb_t_kernel(tc, task_h, share_h, ews1, ebs1, ew1, eb1, gate_pr
                 in_=w_grouped[:, s].rearrange("q g c t -> q (g c t)"),
             )
 
-        for step in range(UNITS + 2):
+        CLOSE = UNITS - 2 * STREAMS
+
+        def matmul_until(step):
+            return step - 2
+
+        def relu_until(step):
+            return matmul_until(step - 1)
+
+        def back_until(step):
+            return relu_until(step) if step > CLOSE else relu_until(step - 1)
+
+        def weigh_until(step):
+            return back_until(step) if step >= CLOSE else back_until(step - 1)
+
+        def sum_until(step):
+            done = weigh_until(step - 1)
+            if step < CLOSE and weigh_until(step) % STREAMS == 0:
+                done -= 1
+            return done
+
+        def newly(until, step):
+            return range(max(until(step - 1) + 1, 0), until(step) + 1)
+
+        for step in range(UNITS):
             if step > 0 and step + AHEAD - 1 < UNITS:
                 load(step + AHEAD - 1)
-            if 0 <= step - 2:
-                bias_relu(step - 2)
-            if step < UNITS:
-                transpose_in(step)
-            if 0 <= step - 2:
-                transpose_back(step - 2)
-            if 0 <= step - 1 < UNITS:
+            for n in newly(relu_until, step):
+                bias_relu(n)
+            transpose_in(step)
+            for n in newly(back_until, step):
+                transpose_back(n)
+            if step > 0:
                 quantise(step - 1)
             if step == 1:
                 group_weights(0, nc.vector.tensor_copy)
                 spread_biases()
             if 1 <= step <= STREAMS:
                 quantise_weights(step - 1)
-            if 0 <= step - 1 < UNITS:
-                expert_matmul(step - 1)
+            for n in newly(matmul_until, step):
+                expert_matmul(n)
             if step == 2:
                 gate_logits(nc.vector, 0, 1)
                 gate_logits(nc.gpsimd, 1, CHUNKS)
@@ -297,15 +339,18 @@ def tile_plelayer_pb_t_kernel(tc, task_h, share_h, ews1, ebs1, ew1, eb1, gate_pr
             if step == 6:
                 gate_total(1, CHUNKS)
                 gate_divide(nc.gpsimd, 1, CHUNKS)
-            closer = step > UNITS - STREAMS
-            if closer and step == UNITS - STREAMS + 1:
-                sum_experts(step - 4)
-            sum_unit, weigh_unit = (step - 3, step - 2) if closer else (step - 4, step - 3)
-            if step == UNITS - STREAMS:
-                weigh(weigh_unit)
-                weigh_unit += 1
-            if 0 <= sum_unit:
-                sum_experts(sum_unit)
-            if 0 <= weigh_unit:
-                weigh(weigh_unit)
-        sum_experts(UNITS - 1)
+            for n in newly(weigh_until, step):
+                weigh(n)
+            for n in newly(sum_until, step):
+                sum_experts(n)
+
+        last = UNITS - 1
+        quantise(last)
+        for n in range(relu_until(last) + 1, UNITS):
+            if n < last:
+                expert_matmul(n + 1)
+            bias_relu(n)
+            transpose_back(n)
+            weigh(n)
+            sum_experts(n - 1)
+        sum_experts(last)

@@ -83,16 +83,16 @@ def tile_plelayer_pb_t_kernel(tc, task_h, share_h, ews1, ebs1, ew1, eb1, gate_pr
             )
 
         load(0, pieces=J)
-        load(1)
+        load(1, pieces=2)
         load_weights(0)
-        load_weights(1)
         load(2)
+        load_weights(1)
+        load(3)
         gate_raw = const.tile([P, T, ROWS * G], BF16)
         nc.sync.dma_start(out=gate_raw[:], in_=gate_pre1.rearrange("t (p j) g -> p t (j g)", p=P))
         load_weights(2)
-        load(3)
-        load_weights(3)
         load(4)
+        load_weights(3)
 
         def rows_of(n):
             return UNIT_LIST[n][3] - UNIT_LIST[n][2]
@@ -179,7 +179,9 @@ def tile_plelayer_pb_t_kernel(tc, task_h, share_h, ews1, ebs1, ew1, eb1, gate_pr
                 )
                 own = own.rearrange("p j v e -> p (j v e)")
                 shared = shared_tiles[chunk][:, s - 1, row:end].rearrange("p j v e -> p (j v e)")
-                nc.gpsimd.tensor_tensor(out=own, in0=own, in1=shared, op=ALU.add)
+                at_the_ends = chunk == 0 or (chunk == CHUNKS - 1 and s >= T - 1)
+                adder = nc.vector if at_the_ends else nc.gpsimd
+                adder.tensor_tensor(out=own, in0=own, in1=shared, op=ALU.add)
 
         def sum_experts(n):
             chunk, s, row, end = UNIT_LIST[n]
@@ -314,29 +316,32 @@ def tile_plelayer_pb_t_kernel(tc, task_h, share_h, ews1, ebs1, ew1, eb1, gate_pr
                 transpose_back(n)
             if step > 0:
                 quantise(step - 1)
+            if step == UNITS - 1:
+                quantise(step)
             if step == 1:
                 group_weights(0, nc.vector.tensor_copy)
                 spread_biases()
-            if 1 <= step <= STREAMS:
-                quantise_weights(step - 1)
+                quantise_weights(0)
+            if 3 <= step <= STREAMS + 1:
+                quantise_weights(step - 2)
             for n in newly(matmul_until, step):
                 expert_matmul(n)
-            if step == 2:
+            if 2 <= step <= STREAMS:
+                group_weights(step - 1)
+            if step == 3:
                 gate_logits(nc.vector, 0, 1)
                 gate_logits(nc.gpsimd, 1, CHUNKS)
                 gate_maximum(0, 1)
                 gate_shift(nc.vector, 0, 1)
                 gate_exp(0, 1)
-            if 1 <= step < STREAMS:
-                group_weights(step)
-            if step == 3:
+            if step == 4:
                 gate_total(0, 1)
                 gate_divide(nc.vector, 0, 1)
                 gate_maximum(1, CHUNKS)
                 gate_shift(nc.gpsimd, 1, CHUNKS)
-            if step == 5:
-                gate_exp(1, CHUNKS)
             if step == 6:
+                gate_exp(1, CHUNKS)
+            if step == 7:
                 gate_total(1, CHUNKS)
                 gate_divide(nc.gpsimd, 1, CHUNKS)
             for n in newly(weigh_until, step):
@@ -345,7 +350,6 @@ def tile_plelayer_pb_t_kernel(tc, task_h, share_h, ews1, ebs1, ew1, eb1, gate_pr
                 sum_experts(n)
 
         last = UNITS - 1
-        quantise(last)
         for n in range(relu_until(last) + 1, UNITS):
             if n < last:
                 expert_matmul(n + 1)

@@ -49,7 +49,7 @@ def tile_plelayer_pb_t_kernel(tc, task_h, share_h, ews1, ebs1, ew1, eb1, gate_pr
         ctx.enter_context(tc.manual_schedule())
 
         x_tiles, grouped_tiles, code_tiles, scale_tiles = {}, {}, {}, {}
-        acc_tiles, relu_tiles, nat_tiles, own_tiles, shared_tiles = {}, {}, {}, {}, {}
+        acc_tiles, relu_tiles, nat_tiles, prod_tiles = {}, {}, {}, {}
 
         def load(n, pieces=1):
             chunk, stream, row, end = UNIT_LIST[n]
@@ -161,27 +161,20 @@ def tile_plelayer_pb_t_kernel(tc, task_h, share_h, ews1, ebs1, ew1, eb1, gate_pr
             chunk, s, row, end = UNIT_LIST[n]
             values = nat_tiles[n][:, 0 : end - row].rearrange("p j (v e) -> p j v e", v=V)
             if s == 0:
-                own_tiles[chunk] = prod_pool.tile([P, T, J, V, E], F32, name="own")
-                shared_tiles[chunk] = prod_pool.tile([P, T, J, V, E], F32, name="shared")
+                prod_tiles[chunk] = prod_pool.tile([P, T, J, V, G], F32, name="prod")
                 nc.vector.tensor_tensor(
-                    out=shared_tiles[chunk][:],
+                    out=prod_tiles[chunk][:, :, :, :, E:G],
                     in0=values.unsqueeze(1).to_broadcast([P, T, J, V, E]),
                     in1=gate[:, chunk, 1].unsqueeze(3).to_broadcast([P, T, J, V, E]),
                     op=ALU.mult,
                 )
             else:
-                own = own_tiles[chunk][:, s - 1, row:end]
                 nc.vector.tensor_tensor(
-                    out=own,
+                    out=prod_tiles[chunk][:, s - 1, row:end, :, 0:E],
                     in0=values,
                     in1=gate[:, chunk, 0, s - 1, row:end].unsqueeze(2).to_broadcast([P, end - row, V, E]),
                     op=ALU.mult,
                 )
-                own = own.rearrange("p j v e -> p (j v e)")
-                shared = shared_tiles[chunk][:, s - 1, row:end].rearrange("p j v e -> p (j v e)")
-                at_the_ends = chunk == 0 or (chunk == CHUNKS - 1 and s >= T - 1)
-                adder = nc.vector if at_the_ends else nc.gpsimd
-                adder.tensor_tensor(out=own, in0=own, in1=shared, op=ALU.add)
 
         def sum_experts(n):
             chunk, s, row, end = UNIT_LIST[n]
@@ -190,7 +183,7 @@ def tile_plelayer_pb_t_kernel(tc, task_h, share_h, ews1, ebs1, ew1, eb1, gate_pr
             cols = slice((chunk * J + row) * V, (chunk * J + end) * V)
             nc.vector.tensor_reduce(
                 out=out_sb[:, s - 1, cols],
-                in_=own_tiles[chunk][:, s - 1, row:end].rearrange("p j v e -> p (j v) e"),
+                in_=prod_tiles[chunk][:, s - 1, row:end].rearrange("p j v g -> p (j v) g"),
                 axis=AX.X,
                 op=ALU.add,
             )

from contextlib import ExitStack

import concourse.mybir as mybir
from concourse.masks import make_identity

F32 = mybir.dt.float32
BF16 = mybir.dt.bfloat16
U32 = mybir.dt.uint32
U8 = mybir.dt.uint8
FP8X4 = mybir.dt.float8_e4m3fn_x4
ACT = mybir.ActivationFunctionType
ALU = mybir.AluOpType
AX = mybir.AxisListType

P = 128
T, B, U, V, E = 3, 4096, 1024, 16, 8
G = 2 * E
C = V * E
STREAMS = T + 1
PACK = 4
K_PASS = P * PACK
PASSES = U // K_PASS
ROWS = B // P
J = 4
CHUNKS = ROWS // J
WHOLE_UNITS = [(c, s, 0, J) for c in range(CHUNKS) for s in range(STREAMS)][:-1]
UNIT_LIST = WHOLE_UNITS + [(CHUNKS - 1, T, 0, J // 2), (CHUNKS - 1, T, J // 2, J)]
UNITS = len(UNIT_LIST)
WORDS = U // 2
AHEAD = 5

FLOPS = 2 * STREAMS * B * U * C


def tile_plelayer_pb_t_kernel(tc, task_h, share_h, ews1, ebs1, ew1, eb1, gate_pre1, gb1, out):
    nc = tc.nc
    stream_rows = [share_h.rearrange("(p j) u -> p (j u)", p=P)]
    stream_rows += [task_h[t].rearrange("(p j) u -> p (j u)", p=P) for t in range(T)]
    out_rows = out.rearrange("t (p j) v -> p t (j v)", p=P)

    with ExitStack() as ctx:
        const = ctx.enter_context(tc.tile_pool(name="const", bufs=1))
        x_pool = ctx.enter_context(tc.tile_pool(name="x", bufs=AHEAD + 1))
        mx_pool = ctx.enter_context(tc.tile_pool(name="mx", bufs=4))
        prod_pool = ctx.enter_context(tc.tile_pool(name="prod", bufs=2))
        fwd_ps = ctx.enter_context(tc.psum_pool(name="fwd", bufs=4))
        acc_ps = ctx.enter_context(tc.psum_pool(name="acc", bufs=2))
        nat_ps = ctx.enter_context(tc.psum_pool(name="nat", bufs=2))
        ctx.enter_context(tc.manual_schedule())

        x_tiles, grouped_tiles, code_tiles, scale_tiles = {}, {}, {}, {}
        acc_tiles, relu_tiles, nat_tiles, prod_tiles = {}, {}, {}, {}

        def load(n, pieces=1):
            chunk, stream, row, end = UNIT_LIST[n]
            x_tiles[n] = x_pool.tile([P, J * U], BF16, name="x_rows")
            width = (end - row) * U // pieces
            for i in range(pieces):
                first = (chunk * J + row) * U + i * width
                nc.sync.dma_start(
                    out=x_tiles[n][:, i * width : (i + 1) * width], in_=stream_rows[stream][:, first : first + width]
                )

        bias_rows = const.tile([P, P], BF16)
        nc.vector.memset(bias_rows[:], 0.0)
        gate_bias_row = const.tile([P, T * G], BF16)
        nc.vector.memset(gate_bias_row[:], 0.0)
        nc.scalar.dma_start(out=bias_rows[0:1, :], in_=ebs1.rearrange("v x -> (v x)").unsqueeze(0))
        nc.scalar.dma_start(out=bias_rows[1:STREAMS, :], in_=eb1.rearrange("t v x -> t (v x)"))
        nc.scalar.dma_start(out=gate_bias_row[0:1, :], in_=gb1.rearrange("t g -> (t g)").unsqueeze(0))
        warm = const.tile([P, 1], F32)
        nc.gpsimd.memset(warm[:], 0.0)
        nc.scalar.activation(out=warm[:], in_=warm[:], func=ACT.Exp)
        ident = const.tile([P, P], F32)
        make_identity(nc, ident[:])
        w_raw = const.tile([P, STREAMS, PASSES, PACK, C], BF16)

        def load_weights(s):
            w_hbm = ews1 if s == 0 else ew1[s - 1]
            nc.sync.dma_start(
                out=w_raw[:, s].rearrange("q g t c -> q g (t c)"),
                in_=w_hbm.rearrange("(g q t) v x -> q g (t v x)", g=PASSES, q=P, t=PACK),
            )

        load(0, pieces=J)
        load(1, pieces=2)
        load_weights(0)
        load(2)
        load_weights(1)
        load(3)
        gate_raw = const.tile([P, T, ROWS * G], BF16)
        nc.sync.dma_start(out=gate_raw[:], in_=gate_pre1.rearrange("t (p j) g -> p t (j g)", p=P))
        load_weights(2)
        load(4)
        load_weights(3)

        def rows_of(n):
            return UNIT_LIST[n][3] - UNIT_LIST[n][2]

        def transpose_in(n):
            x_words = x_tiles[n][:].bitcast(F32)
            grouped_tiles[n] = mx_pool.tile([P, PASSES * J * P * PACK], BF16, name="grouped", align_bytes=64)
            cols = rows_of(n) * P
            grouped_words = grouped_tiles[n][:, 0 : PASSES * cols * PACK].bitcast(F32)
            grouped_words = grouped_words.rearrange("q (g c h) -> q g c h", g=PASSES, h=2)
            for j in range(rows_of(n)):
                xt = fwd_ps.tile([P, 4, P], F32, name="xt")
                for g in range(PASSES):
                    for h in range(2):
                        first = j * WORDS + g * 2 * P + h
                        last = j * WORDS + (g + 1) * 2 * P
                        nc.tensor.transpose(xt[:, 2 * g + h, :], x_words[:, first:last:2], ident[:])
                nc.scalar.copy(
                    out=grouped_words[:, :, j * P : (j + 1) * P, :],
                    in_=xt[:].rearrange("q (g h) r -> q g r h", g=PASSES),
                )

        def quantise(n):
            code_tiles[n] = mx_pool.tile([P, PASSES * J * P], U32, name="codes", align_bytes=64)
            scale_tiles[n] = mx_pool.tile([P, PASSES * J * P], U8, name="scales", align_bytes=64)
            cols = PASSES * rows_of(n) * P
            nc.vector.quantize_mx(
                out=code_tiles[n][:, 0:cols].bitcast(FP8X4),
                scales=scale_tiles[n][:, 0:cols],
                in_=grouped_tiles[n][:, 0 : cols * PACK],
            )

        def expert_matmul(n):
            s = UNIT_LIST[n][1]
            cols = rows_of(n) * P
            acc_tiles[n] = acc_ps.tile([P, J * P], F32, name="acc")
            for g in range(PASSES):
                nc.tensor.matmul_mx(
                    out=acc_tiles[n][:, 0:cols],
                    lhsT=w_codes[:, s, g, :].bitcast(FP8X4),
                    lhsT_scale=w_scales[:, s, g, :],
                    rhs=code_tiles[n][:, g * cols : (g + 1) * cols].bitcast(FP8X4),
                    rhs_scale=scale_tiles[n][:, g * cols : (g + 1) * cols],
                    start=(g == 0),
                    stop=(g == PASSES - 1),
                )

        def bias_relu(n):
            s = UNIT_LIST[n][1]
            cols = rows_of(n) * P
            relu_tiles[n] = mx_pool.tile([P, J * P], F32, name="relu")
            nc.scalar.activation(
                out=relu_tiles[n][:, 0:cols],
                in_=acc_tiles[n][:, 0:cols],
                func=ACT.Relu,
                bias=bias_col[:, s : s + 1],
                scale=1.0,
            )

        def transpose_back(n):
            nat_tiles[n] = nat_ps.tile([P, J, C], F32, name="nat")
            for j in range(rows_of(n)):
                nc.tensor.transpose(nat_tiles[n][:, j, :], relu_tiles[n][:, j * P : (j + 1) * P], ident[:])

        def weigh(n):
            chunk, s, row, end = UNIT_LIST[n]
            values = nat_tiles[n][:, 0 : end - row].rearrange("p j (v e) -> p j v e", v=V)
            if s == 0:
                prod_tiles[chunk] = prod_pool.tile([P, T, J, V, G], F32, name="prod")
                nc.vector.tensor_tensor(
                    out=prod_tiles[chunk][:, :, :, :, E:G],
                    in0=values.unsqueeze(1).to_broadcast([P, T, J, V, E]),
                    in1=gate[:, chunk, 1].unsqueeze(3).to_broadcast([P, T, J, V, E]),
                    op=ALU.mult,
                )
            else:
                nc.vector.tensor_tensor(
                    out=prod_tiles[chunk][:, s - 1, row:end, :, 0:E],
                    in0=values,
                    in1=gate[:, chunk, 0, s - 1, row:end].unsqueeze(2).to_broadcast([P, end - row, V, E]),
                    op=ALU.mult,
                )

        def sum_experts(n):
            chunk, s, row, end = UNIT_LIST[n]
            if s == 0:
                return
            cols = slice((chunk * J + row) * V, (chunk * J + end) * V)
            nc.vector.tensor_reduce(
                out=out_sb[:, s - 1, cols],
                in_=prod_tiles[chunk][:, s - 1, row:end].rearrange("p j v g -> p (j v) g"),
                axis=AX.X,
                op=ALU.add,
            )
            if chunk == CHUNKS - 1:
                nc.sync.dma_start(out=out_rows[:, s - 1, cols], in_=out_sb[:, s - 1, cols])
            elif s == T:
                nc.sync.dma_start(out=out_rows[:, :, cols], in_=out_sb[:, :, cols])

        out_sb = const.tile([P, T, ROWS * V], F32)

        gate_bias = const.tile([P, T, G], F32)
        bias_col = const.tile([P, STREAMS], F32)
        ones = const.tile([P, P], BF16)
        nc.vector.memset(ones[:], 1.0)
        bias_rows_f32 = const.tile([P, P], F32)

        def spread_biases():
            nc.vector.tensor_copy(out=bias_rows_f32[:], in_=bias_rows[:])
            gb_ps = acc_ps.tile([P, J * P], F32, name="acc")
            nc.tensor.matmul(gb_ps[:, 0 : T * G], lhsT=ones[:], rhs=gate_bias_row[:], start=True, stop=True)
            bias_ps = nat_ps.tile([P, J, C], F32, name="nat")
            nc.tensor.transpose(bias_ps[:, 0, :], bias_rows_f32[:], ident[:])
            nc.vector.tensor_copy(out=bias_col[:], in_=bias_ps[:, 0, 0:STREAMS])
            nc.vector.tensor_copy(out=gate_bias[:].rearrange("p t g -> p (t g)"), in_=gb_ps[:, 0 : T * G])

        logits = const.tile([P, CHUNKS, T, J, G], F32)
        gate = const.tile([P, CHUNKS, 2, T, J, E], F32)
        gate_max = const.tile([P, CHUNKS * T * J], F32)
        gate_sum = const.tile([P, CHUNKS * T * J], F32)

        def gate_rows(tile, first, last):
            return tile[:, first * T * J : last * T * J].unsqueeze(2).to_broadcast([P, (last - first) * T * J, G])

        def gate_logits(eng, first, last):
            for t in range(T):
                eng.tensor_tensor(
                    out=logits[:, first:last, t],
                    in0=gate_raw[:, t, first * J * G : last * J * G].rearrange("p (c j g) -> p c j g", j=J, g=G),
                    in1=gate_bias[:, t, :].unsqueeze(1).unsqueeze(1).to_broadcast([P, last - first, J, G]),
                    op=ALU.add,
                )

        def flat_logits(first, last):
            return logits[:, first:last].rearrange("p c t j g -> p (c t j) g")

        def gate_maximum(first, last):
            nc.vector.tensor_reduce(
                out=gate_max[:, first * T * J : last * T * J], in_=flat_logits(first, last), axis=AX.X, op=ALU.max
            )

        def gate_shift(eng, first, last):
            eng.tensor_tensor(
                out=flat_logits(first, last),
                in0=flat_logits(first, last),
                in1=gate_rows(gate_max, first, last),
                op=ALU.subtract,
            )

        def gate_exp(first, last):
            nc.scalar.activation(out=flat_logits(first, last), in_=flat_logits(first, last), func=ACT.Exp)

        def gate_total(first, last):
            rows = slice(first * T * J, last * T * J)
            nc.vector.tensor_reduce(out=gate_sum[:, rows], in_=flat_logits(first, last), axis=AX.X, op=ALU.add)
            nc.vector.reciprocal(out=gate_sum[:, rows], in_=gate_sum[:, rows])

        def gate_divide(eng, first, last):
            for half in range(2):
                eng.tensor_tensor(
                    out=gate[:, first:last, half].rearrange("p c t j e -> p c (t j) e"),
                    in0=logits[:, first:last, :, :, half * E : (half + 1) * E].rearrange("p c t j e -> p c (t j) e"),
                    in1=gate_sum[:, first * T * J : last * T * J]
                    .rearrange("p (c r) -> p c r", r=T * J)
                    .unsqueeze(3)
                    .to_broadcast([P, last - first, T * J, E]),
                    op=ALU.mult,
                )

        w_grouped = const.tile([P, STREAMS, PASSES, C, PACK], BF16, align_bytes=64)
        w_codes = const.tile([P, STREAMS, PASSES, C], U32, align_bytes=64)
        w_scales = const.tile([P, STREAMS, PASSES, C], U8, align_bytes=64)

        def group_weights(s, copy=nc.scalar.copy):
            copy(out=w_grouped[:, s], in_=w_raw[:, s].rearrange("q g t c -> q g c t"))

        def quantise_weights(s):
            nc.vector.quantize_mx(
                out=w_codes[:, s].rearrange("q g c -> q (g c)").bitcast(FP8X4),
                scales=w_scales[:, s].rearrange("q g c -> q (g c)"),
                in_=w_grouped[:, s].rearrange("q g c t -> q (g c t)"),
            )

        CLOSE = UNITS - 2 * STREAMS

        def matmul_until(step):
            return step - 2

        def relu_until(step):
            return matmul_until(step - 1)

        def back_until(step):
            return relu_until(step) if step > CLOSE else relu_until(step - 1)

        def weigh_until(step):
            return back_until(step) if step >= CLOSE else back_until(step - 1)

        def sum_until(step):
            done = weigh_until(step - 1)
            if step < CLOSE and weigh_until(step) % STREAMS == 0:
                done -= 1
            return done

        def newly(until, step):
            return range(max(until(step - 1) + 1, 0), until(step) + 1)

        for step in range(UNITS):
            if step > 0 and step + AHEAD - 1 < UNITS:
                load(step + AHEAD - 1)
            for n in newly(relu_until, step):
                bias_relu(n)
            transpose_in(step)
            for n in newly(back_until, step):
                transpose_back(n)
            if step > 0:
                quantise(step - 1)
            if step == UNITS - 1:
                quantise(step)
            if step == 1:
                group_weights(0, nc.vector.tensor_copy)
                spread_biases()
                quantise_weights(0)
            if 3 <= step <= STREAMS + 1:
                quantise_weights(step - 2)
            for n in newly(matmul_until, step):
                expert_matmul(n)
            if 2 <= step <= STREAMS:
                group_weights(step - 1)
            if step == 3:
                gate_logits(nc.vector, 0, 1)
                gate_logits(nc.gpsimd, 1, CHUNKS)
                gate_maximum(0, 1)
                gate_shift(nc.vector, 0, 1)
                gate_exp(0, 1)
            if step == 4:
                gate_total(0, 1)
                gate_divide(nc.vector, 0, 1)
                gate_maximum(1, CHUNKS)
                gate_shift(nc.gpsimd, 1, CHUNKS)
            if step == 6:
                gate_exp(1, CHUNKS)
            if step == 7:
                gate_total(1, CHUNKS)
                gate_divide(nc.gpsimd, 1, CHUNKS)
            for n in newly(weigh_until, step):
                weigh(n)
            for n in newly(sum_until, step):
                sum_experts(n)

        last = UNITS - 1
        for n in range(relu_until(last) + 1, UNITS):
            if n < last:
                expert_matmul(n + 1)
            bias_relu(n)
            transpose_back(n)
            weigh(n)
            sum_experts(n - 1)
        sum_experts(last)
